import numpy as np
import ml_dtypes


def mxq(x, axis, fmt="e4m3"):
    dtype, down = {"e4m3": (ml_dtypes.float8_e4m3fn, 7), "e5m2": (ml_dtypes.float8_e5m2, 14)}[fmt]
    v = np.moveaxis(np.asarray(x, np.float32).astype(ml_dtypes.bfloat16).astype(np.float64), axis, -1)
    blocks = v.reshape(v.shape[:-1] + (-1, 32))
    amax = np.abs(blocks).max(-1, keepdims=True)
    byte = np.maximum(np.where(amax > 0, np.frexp(amax)[1] - 1 + 127, 0) - down, 1)
    scale = np.exp2(byte - 127.0)
    codes = (blocks / scale).astype(np.float32).astype(dtype).astype(np.float64)
    return np.moveaxis((codes * scale).reshape(v.shape), -1, axis)


WIDE = False


def mx_kscale(k):
    if not WIDE:
        return np.ones(k)
    levels = np.array([10, -10, 5, -5, 0])
    a = np.random.permutation(np.resize(levels, k // 512 * 4)).reshape(k // 512, 4)
    idx = np.arange(k)
    return np.exp2(a[idx // 512, idx % 128 // 32])


BF16 = ml_dtypes.bfloat16


def bf(x):
    return np.asarray(x, np.float32).astype(BF16)


def f64(x):
    return np.asarray(x).astype(np.float64)


B, L, H, E, WINDOW, QB = 1, 1024, 16, 128, 512, 512
MXB = 32


def alibi_slopes():
    return np.exp2(-8.0 * (np.arange(H) + 1.0) / H)


def setup_inputs():
    z = np.random.standard_normal((B, L, 3, H, E))
    z[:, :, 2] *= (0.5 / np.sqrt(alibi_slopes()))[:, None]
    s = mx_kscale(L)
    t = np.where((np.arange(L) // MXB) % 2 == 0, s.min(), s) / s.min()
    hs = slice(H // 2, H)
    z[:, :, 2, hs] *= t[None, :, None, None]
    z[:, :, 0, hs, 0] = np.sqrt(E) * np.log(2.0)
    z[:, :, 1, hs, 0] -= np.log2(t)[None, :, None]
    return {"qkv": bf(z)}


def reference(qkv):
    qkv = f64(qkv)
    q = qkv[:, :, 0].transpose(0, 2, 1, 3)
    k = qkv[:, :, 1].transpose(0, 2, 1, 3)
    vq = mxq(qkv[:, :, 2].transpose(0, 2, 1, 3), 2, "e4m3")
    slopes = alibi_slopes()
    outs = []
    for q0 in range(0, L, QB):
        q1 = q0 + QB
        k0 = max(0, q0 - WINDOW)
        s = q[:, :, q0:q1] @ k[:, :, k0:q1].transpose(0, 1, 3, 2) * (1.0 / E ** 0.5)
        dist = np.arange(q0, q1)[:, None] - np.arange(k0, q1)[None, :]
        s = s - slopes[None, :, None, None] * dist
        s = np.where((dist >= 0) & (dist < WINDOW), s, -np.inf)
        e = np.exp(s - s.max(-1, keepdims=True))
        outs.append((mxq(e, 3, "e4m3") @ vq[:, :, k0:q1]) / e.sum(-1, keepdims=True))
    return np.concatenate(outs, 2).transpose(0, 2, 1, 3)

@@ -1,0 +1,359 @@
+from contextlib import ExitStack
+import math
+
+import concourse.mybir as mybir
+from concourse.masks import make_identity
+
+F32 = mybir.dt.float32
+BF16 = mybir.dt.bfloat16
+U32 = mybir.dt.uint32
+U8 = mybir.dt.uint8
+FP8X4 = mybir.dt.float8_e4m3fn_x4
+ALU = mybir.AluOpType
+ACT = mybir.ActivationFunctionType
+AX = mybir.AxisListType
+
+P = 128
+H = 16
+L = 1024
+E = 128
+NQB = L // P
+GH = 4
+NG = NQB * H // GH
+NT = NQB * H
+SCALE = 1.0 / math.sqrt(E)
+MASKED = 1.0e30
+FLOPS = 4 * E * H * (512 * 512 + 512 * 1024)
+
+VEC_EVAC = (0, 3, 6)
+
+
+def tile_flexattention_kernel(tc, qkv, out):
+    nc = tc.nc
+    with ExitStack() as ctx:
+        ctx.enter_context(tc.manual_schedule())
+        const = ctx.enter_context(tc.tile_pool(name="const", bufs=1))
+        ld = ctx.enter_context(tc.tile_pool(name="ld", bufs=4))
+        qpool = ctx.enter_context(tc.tile_pool(name="qpool", bufs=3))
+        vpool = ctx.enter_context(tc.tile_pool(name="vpool", bufs=2))
+        small = ctx.enter_context(tc.tile_pool(name="small", bufs=8))
+        gsmall = ctx.enter_context(tc.tile_pool(name="gsmall", bufs=6))
+        epool = ctx.enter_context(tc.tile_pool(name="epool", bufs=4))
+        gpool = ctx.enter_context(tc.tile_pool(name="gpool", bufs=4))
+        cpool = ctx.enter_context(tc.tile_pool(name="cpool", bufs=12))
+        opool = ctx.enter_context(tc.tile_pool(name="opool", bufs=3))
+        ps_s = ctx.enter_context(tc.psum_pool(name="ps_s", bufs=3))
+        ps_w = ctx.enter_context(tc.psum_pool(name="ps_w", bufs=2))
+        ps_t = ctx.enter_context(tc.psum_pool(name="ps_t", bufs=1))
+        ps_x = ctx.enter_context(tc.psum_pool(name="ps_x", bufs=1))
+
+        xs = {}
+        vraw = const.tile([P, NQB, H * E], BF16, name="vraw")
+        vsrc = qkv[0, :, 2].rearrange("(k p) h e -> p k (h e)", p=P)
+
+        def load_x(pb):
+            x = ld.tile([P, 2 * H * E], BF16, tag="x", name="x")
+            nc.sync.dma_start(
+                out=x[:],
+                in_=qkv[0, pb * P : (pb + 1) * P, 0:2].rearrange("p w h e -> p (w h e)"),
+            )
+            xs[pb] = x
+
+        load_x(0)
+        nc.sync.dma_start(out=vraw[:, 0:4, :], in_=vsrc[:, 0:4, :])
+        for pb in range(1, 4):
+            load_x(pb)
+        nc.sync.dma_start(out=vraw[:, 4:8, :], in_=vsrc[:, 4:8, :])
+
+        ident_bf = const.tile([P, P], BF16, name="ident_bf")
+        make_identity(nc, ident_bf[:])
+        ident_f = const.tile([P, P], F32, name="ident_f")
+        make_identity(nc, ident_f[:])
+        zero_bf = const.tile([P, P], BF16, name="zero_bf")
+        nc.vector.memset(zero_bf[:], 0.0)
+        dist_t = const.tile([P, 5, P], F32, name="dist_t")
+        nc.gpsimd.iota(
+            dist_t[:],
+            pattern=[[P, 5], [1, P]],
+            base=0,
+            channel_multiplier=-1,
+            allow_small_or_imprecise_dtypes=True,
+        )
+        nc.gpsimd.affine_select(
+            out=dist_t[:, 0, :], in_=dist_t[:, 0, :], pattern=[[1, P]],
+            compare_op=ALU.is_ge, fill=MASKED, base=0, channel_multiplier=-1,
+        )
+        nc.gpsimd.affine_select(
+            out=dist_t[:, 4, :], in_=dist_t[:, 4, :], pattern=[[-1, P]],
+            compare_op=ALU.is_gt, fill=MASKED, base=0, channel_multiplier=1,
+        )
+        bias_t = const.tile([P, H, 5, P], F32, name="bias_t")
+        k_t = const.tile([P, H, L], BF16, name="k_t")
+        vcodes = const.tile([P, 2, H * E], U32, name="vcodes", align_bytes=64)
+        vscales = const.tile([P, 2, H * E], U8, name="vscales", align_bytes=64)
+        tps = [
+            ps_t.tile([P, 8, P], BF16, name="tp0"),
+            ps_t.tile([P, 8, P], BF16, name="tp1"),
+        ]
+        tp_zero = [[False] * 8, [False] * 8]
+        counters = {"tp": 0, "evac": 0}
+        st = {}
+
+        def where(n):
+            qb = n // H
+            return qb, (n % H) // GH, n % GH, n % H
+
+        def prepare_bank(live):
+            i = counters["tp"] % 2
+            counters["tp"] += 1
+            for s in range(8):
+                if s in live:
+                    tp_zero[i][s] = False
+                elif not tp_zero[i][s]:
+                    nc.tensor.transpose(tps[i][:, s, :], zero_bf[:], ident_bf[:])
+                    tp_zero[i][s] = True
+            return tps[i]
+
+        def g_bias(g):
+            for h in range(GH * (g % 4), GH * (g % 4) + GH):
+                sigma = 2.0 ** (-(h + 1) / 2.0) * math.sqrt(E)
+                nc.vector.tensor_scalar(
+                    out=bias_t[:, h], in0=dist_t[:], scalar1=-sigma, scalar2=None, op0=ALU.mult
+                )
+
+        def g_qk_transpose(g):
+            qb, hg = g // 4, g % 4
+            qk_ps = ps_x.tile([P, 8, P], BF16, tag="x", name="qk_ps")
+            for j in range(GH):
+                h = GH * hg + j
+                nc.tensor.transpose(qk_ps[:, j, :], xs[qb][:, h * E : (h + 1) * E], ident_bf[:])
+                nc.tensor.transpose(
+                    qk_ps[:, GH + j, :], xs[qb][:, (H + h) * E : (H + h + 1) * E], ident_bf[:]
+                )
+            st["qk_ps", g] = qk_ps
+
+        def g_qk_copy(g):
+            qb, hg = g // 4, g % 4
+            qk_ps = st["qk_ps", g]
+            q_t = qpool.tile([P, GH, P], BF16, tag="q_t", name="q_t")
+            nc.scalar.copy(out=q_t[:], in_=qk_ps[:, 0:GH, :])
+            nc.scalar.copy(
+                out=k_t[:, GH * hg : GH * hg + GH, qb * P : (qb + 1) * P], in_=qk_ps[:, GH : 2 * GH, :]
+            )
+            st["q_t", g] = q_t
+
+        def g_v(g):
+            c, hg = g // 16, g % 4
+            cols = slice(hg * GH * E, (hg + 1) * GH * E)
+            gv = vpool.tile([P, GH * E, 4], BF16, tag="gv", name="gv", align_bytes=64)
+            nc.vector.tensor_copy(
+                out=gv[:].rearrange("p (c i) t -> p c t i", i=4),
+                in_=vraw[:, 4 * c : 4 * c + 4, cols].rearrange("p t (c i) -> p c t i", i=4),
+            )
+            st["gv", g] = gv
+
+        def g_v_quantise(g):
+            c, hg = g // 16, g % 4
+            cols = slice(hg * GH * E, (hg + 1) * GH * E)
+            gv = st["gv", g]
+            nc.vector.quantize_mx(
+                out=vcodes[:, c, cols].bitcast(FP8X4),
+                scales=vscales[:, c, cols],
+                in_=gv[:].rearrange("p x t -> p (x t)"),
+            )
+
+        def g_window_scores(g):
+            qb, hg = g // 4, g % 4
+            wb = ps_w.tile([P, GH, P], F32, tag="w", name="wb")
+            q_t = st["q_t", g]
+            for j in range(GH):
+                h = GH * hg + j
+                nc.tensor.matmul(
+                    wb[:, j, :], lhsT=bias_t[:, h, 4, :], rhs=ident_f[:],
+                    is_transpose=True, start=True, stop=False,
+                )
+                nc.tensor.matmul(
+                    wb[:, j, :], lhsT=q_t[:, j, :], rhs=k_t[:, h, (qb - 4) * P : (qb - 3) * P],
+                    start=False, stop=True,
+                )
+            st["wb", g] = wb
+
+        def g_window_max(g):
+            mw = gsmall.tile([P, GH], F32, tag="mw", name="mw")
+            nc.vector.tensor_reduce(out=mw[:], in_=st["wb", g][:], axis=AX.X, op=ALU.max)
+            st["mw", g] = mw
+
+        def g_mx(g):
+            qb, hg = g // 4, g % 4
+            ob = ps_x.tile([P, GH, P], F32, tag="x", name="ob")
+            for j in range(GH):
+                h = GH * hg + j
+                fcols = slice(h * E, (h + 1) * E)
+                if qb >= 4:
+                    codes, scl = st["codes", GH * g + j]
+                    passes = [(0, 0), (1, 1)]
+                else:
+                    codes, scl = st["codes", GH * g + (j // 2) * 2 + 1]
+                    passes = [(j % 2, 0)]
+                for i, (half, c) in enumerate(passes):
+                    qcols = slice(half * P, (half + 1) * P)
+                    nc.tensor.matmul_mx(
+                        out=ob[:, j, :],
+                        lhsT=codes[:, qcols].bitcast(FP8X4),
+                        lhsT_scale=scl[:, qcols],
+                        rhs=vcodes[:, c, fcols].bitcast(FP8X4),
+                        rhs_scale=vscales[:, c, fcols],
+                        start=(i == 0),
+                        stop=(i == len(passes) - 1),
+                    )
+            st["ob", g] = ob
+
+        def g_out(g):
+            qb, hg = g // 4, g % 4
+            ob = st["ob", g]
+            rs = st["rs", g]
+            rinv = gsmall.tile([P, GH], F32, tag="rinv", name="rinv")
+            if qb >= 4:
+                rt = gsmall.tile([P, GH], F32, tag="rt", name="rt")
+                nc.vector.tensor_reduce(out=rt[:], in_=rs[:], axis=AX.X, op=ALU.add)
+                nc.vector.reciprocal(out=rinv[:], in_=rt[:])
+            else:
+                nc.vector.reciprocal(out=rinv[:], in_=rs[:, :, 0])
+            ost = opool.tile([P, GH, P], F32, tag="ost", name="ost")
+            nc.vector.tensor_tensor(
+                out=ost[:], in0=ob[:], in1=rinv[:].unsqueeze(2).to_broadcast([P, GH, P]), op=ALU.mult
+            )
+            nc.sync.dma_start(out=out[0, qb * P : (qb + 1) * P, GH * hg : GH * hg + GH, :], in_=ost[:])
+
+        def t_scores(n):
+            qb, hg, j, h = where(n)
+            nb = min(qb + 1, 4)
+            sb = ps_s.tile([P, 4 * P], F32, tag="s", name="sb")
+            for b in range(nb):
+                nc.tensor.matmul(
+                    sb[:, b * P : (b + 1) * P], lhsT=bias_t[:, h, nb - 1 - b, :], rhs=ident_f[:],
+                    is_transpose=True, start=(b == 0), stop=False,
+                )
+            nc.tensor.matmul(
+                sb[:, 0 : nb * P], lhsT=st["q_t", n // GH][:, j, :],
+                rhs=k_t[:, h, (qb - nb + 1) * P : (qb + 1) * P], start=False, stop=True,
+            )
+            st["sb", n] = sb
+
+        def t_max(n):
+            qb, hg, j, h = where(n)
+            nb = min(qb + 1, 4)
+            m = small.tile([P, 1], F32, tag="m", name="m")
+            nc.vector.tensor_reduce(out=m[:], in_=st["sb", n][:, 0 : nb * P], axis=AX.X, op=ALU.max)
+            nbias = small.tile([P, 1], F32, tag="nbias", name="nbias")
+            if qb >= 4:
+                nc.vector.tensor_scalar(
+                    out=nbias[:], in0=m[:], scalar1=st["mw", n // GH][:, j : j + 1], scalar2=-SCALE,
+                    op0=ALU.max, op1=ALU.mult,
+                )
+            else:
+                nc.vector.tensor_scalar(out=nbias[:], in0=m[:], scalar1=-SCALE, scalar2=None, op0=ALU.mult)
+            st["nbias", n] = nbias
+
+        def t_exp(n):
+            qb, hg, j, h = where(n)
+            nb = min(qb + 1, 4)
+            g = n // GH
+            if j == 0:
+                st["rs", g] = gsmall.tile([P, GH, 2], F32, tag="rs", name="rs")
+            rs = st["rs", g]
+            nbias = st["nbias", n]
+            sb = st["sb", n]
+            e = epool.tile([P, 5 * P], BF16, tag="e", name="e")
+            nc.scalar.activation(
+                out=e[:, P : P + nb * P], in_=sb[:, 0 : nb * P], func=ACT.Exp,
+                bias=nbias[:], scale=SCALE, accum_out=rs[:, j, 0:1],
+            )
+            if qb >= 4:
+                nc.scalar.activation(
+                    out=e[:, 0:P], in_=st["wb", g][:, j, :], func=ACT.Exp,
+                    bias=nbias[:], scale=SCALE, accum_out=rs[:, j, 1:2],
+                )
+            st["e", n] = e
+
+        def t_transpose(n):
+            qb, hg, j, h = where(n)
+            nb = min(qb + 1, 4)
+            e = st["e", n]
+            if qb >= 4:
+                bank = prepare_bank(set(range(qb - 4, qb + 1)))
+                nc.tensor.transpose(bank[:, qb - 4, :], e[:, 0:P], ident_bf[:])
+                first = qb - 3
+            else:
+                if j % 2 == 0:
+                    st["pair_bank"] = prepare_bank(set(range(nb)) | set(range(4, 4 + nb)))
+                bank = st["pair_bank"]
+                first = 4 * (j % 2)
+            for b in range(nb):
+                nc.tensor.transpose(bank[:, first + b, :], e[:, (1 + b) * P : (2 + b) * P], ident_bf[:])
+            st["bank", n] = bank
+
+        def t_copy(n):
+            qb, hg, j, h = where(n)
+            bank = st["bank", n]
+            if qb < 4 and j % 2 == 0:
+                return
+            grp = gpool.tile([P, 2, P, 4], BF16, tag="grp", name="grp", align_bytes=64)
+            for c in range(2):
+                src = bank[:, 4 * c : 4 * c + 4, :].rearrange("p t q -> p q t")
+                if counters["evac"] % 8 in VEC_EVAC:
+                    nc.vector.tensor_copy(out=grp[:, c], in_=src)
+                else:
+                    nc.scalar.copy(out=grp[:, c], in_=src)
+                counters["evac"] += 1
+            st["grp", n] = grp
+
+        def t_quantise(n):
+            qb, hg, j, h = where(n)
+            if qb < 4 and j % 2 == 0:
+                return
+            grp = st["grp", n]
+            codes = cpool.tile([P, 2 * P], U32, tag="codes", name="codes", align_bytes=64)
+            scl = cpool.tile([P, 2 * P], U8, tag="scl", name="scl", align_bytes=64)
+            nc.vector.quantize_mx(
+                out=codes[:].bitcast(FP8X4), scales=scl[:], in_=grp[:].rearrange("p g q t -> p (g q t)")
+            )
+            st["codes", n] = (codes, scl)
+
+        for s in range(-4, NT + 12):
+            g4, r4 = divmod(s + 4, 4)
+            if 0 <= s < NT:
+                t_scores(s)
+            if 0 <= s - 3 < NT:
+                t_transpose(s - 3)
+            if r4 == 0 and g4 < NG:
+                g_qk_transpose(g4)
+            if r4 == 3 and g4 < NG and g4 >= 16:
+                g_window_scores(g4)
+            gm = (s - 10) // 4
+            if (s - 10) % 4 == 0 and 0 <= gm < NG:
+                g_mx(gm)
+            if r4 == 1 and g4 < 4:
+                g_bias(g4)
+            if r4 == 1 and g4 < NG:
+                g_qk_copy(g4)
+            if s % 4 == 0 and 16 <= s // 4 < NG:
+                g_window_max(s // 4)
+            if 0 <= s - 1 < NT:
+                t_max(s - 1)
+            if 0 <= s - 2 < NT:
+                t_exp(s - 2)
+            if 0 <= s - 4 < NT:
+                t_copy(s - 4)
+            if 0 <= s - 5 < NT:
+                t_quantise(s - 5)
+            gv_g = (s - 2) // 4
+            if (s - 2) % 4 == 0 and 0 <= gv_g < NG and gv_g % 16 < 4:
+                g_v(gv_g)
+            if (s - 3) % 4 == 0 and 0 <= (s - 3) // 4 < NG and ((s - 3) // 4) % 16 < 4:
+                g_v_quantise((s - 3) // 4)
+            go = (s - 11) // 4
+            if (s - 11) % 4 == 0 and 0 <= go < NG:
+                g_out(go)
+            if s % H == 10 and 4 <= s // H + 4 < NQB:
+                load_x(s // H + 4)

@@ -11,7 +11,6 @@ U8 = mybir.dt.uint8
 FP8X4 = mybir.dt.float8_e4m3fn_x4
 ALU = mybir.AluOpType
 ACT = mybir.ActivationFunctionType
-AX = mybir.AxisListType
 
 P = 128
 H = 16
@@ -25,7 +24,12 @@ SCALE = 1.0 / math.sqrt(E)
 MASKED = 1.0e30
 FLOPS = 4 * E * H * (512 * 512 + 512 * 1024)
 
-VEC_EVAC = (0, 3, 6)
+N_TP = 3
+N_X = 3
+VEC_EVAC = (1,)
+GP_BIAS_FROM = 4
+LAG_PASS, LAG_EXP, LAG_TR, LAG_COPY, LAG_Q = 1, 2, 4, 5, 7
+G_QKT, G_QKCOPY, G_BIAS, G_W, G_WPASS, G_V, G_VQ, G_MX, G_OUT = -4, -3, -3, -2, 0, 2, 4, 14, 15
 
 
 def tile_flexattention_kernel(tc, qkv, out):
@@ -33,17 +37,18 @@ def tile_flexattention_kernel(tc, qkv, out):
     with ExitStack() as ctx:
         ctx.enter_context(tc.manual_schedule())
         const = ctx.enter_context(tc.tile_pool(name="const", bufs=1))
-        ld = ctx.enter_context(tc.tile_pool(name="ld", bufs=4))
+        ld = ctx.enter_context(tc.tile_pool(name="ld", bufs=N_X))
         qpool = ctx.enter_context(tc.tile_pool(name="qpool", bufs=3))
         vpool = ctx.enter_context(tc.tile_pool(name="vpool", bufs=2))
         small = ctx.enter_context(tc.tile_pool(name="small", bufs=8))
-        gsmall = ctx.enter_context(tc.tile_pool(name="gsmall", bufs=6))
+        gsmall = ctx.enter_context(tc.tile_pool(name="gsmall", bufs=7))
+        zpool = ctx.enter_context(tc.tile_pool(name="zpool", bufs=8))
         epool = ctx.enter_context(tc.tile_pool(name="epool", bufs=4))
         gpool = ctx.enter_context(tc.tile_pool(name="gpool", bufs=4))
         cpool = ctx.enter_context(tc.tile_pool(name="cpool", bufs=12))
         opool = ctx.enter_context(tc.tile_pool(name="opool", bufs=3))
         ps_s = ctx.enter_context(tc.psum_pool(name="ps_s", bufs=3))
-        ps_w = ctx.enter_context(tc.psum_pool(name="ps_w", bufs=2))
+        ps_w = ctx.enter_context(tc.psum_pool(name="ps_w", bufs=1))
         ps_t = ctx.enter_context(tc.psum_pool(name="ps_t", bufs=1))
         ps_x = ctx.enter_context(tc.psum_pool(name="ps_x", bufs=1))
 
@@ -61,16 +66,12 @@ def tile_flexattention_kernel(tc, qkv, out):
 
         load_x(0)
         nc.sync.dma_start(out=vraw[:, 0:4, :], in_=vsrc[:, 0:4, :])
-        for pb in range(1, 4):
+        for pb in range(1, N_X):
             load_x(pb)
         nc.sync.dma_start(out=vraw[:, 4:8, :], in_=vsrc[:, 4:8, :])
 
         ident_bf = const.tile([P, P], BF16, name="ident_bf")
         make_identity(nc, ident_bf[:])
-        ident_f = const.tile([P, P], F32, name="ident_f")
-        make_identity(nc, ident_f[:])
-        zero_bf = const.tile([P, P], BF16, name="zero_bf")
-        nc.vector.memset(zero_bf[:], 0.0)
         dist_t = const.tile([P, 5, P], F32, name="dist_t")
         nc.gpsimd.iota(
             dist_t[:],
@@ -87,24 +88,24 @@ def tile_flexattention_kernel(tc, qkv, out):
             out=dist_t[:, 4, :], in_=dist_t[:, 4, :], pattern=[[-1, P]],
             compare_op=ALU.is_gt, fill=MASKED, base=0, channel_multiplier=1,
         )
+        ident_f = const.tile([P, P], F32, name="ident_f")
+        make_identity(nc, ident_f[:])
+        zero_bf = const.tile([P, P], BF16, name="zero_bf")
+        nc.vector.memset(zero_bf[:], 0.0)
         bias_t = const.tile([P, H, 5, P], F32, name="bias_t")
         k_t = const.tile([P, H, L], BF16, name="k_t")
         vcodes = const.tile([P, 2, H * E], U32, name="vcodes", align_bytes=64)
         vscales = const.tile([P, 2, H * E], U8, name="vscales", align_bytes=64)
-        tps = [
-            ps_t.tile([P, 8, P], BF16, name="tp0"),
-            ps_t.tile([P, 8, P], BF16, name="tp1"),
-        ]
-        tp_zero = [[False] * 8, [False] * 8]
-        counters = {"tp": 0, "evac": 0}
+        tps = [ps_t.tile([P, 8, P], BF16, name="tp%d" % i) for i in range(N_TP)]
+        tp_zero = [[False] * 8 for i in range(N_TP)]
+        counters = {"tp": 0}
         st = {}
 
         def where(n):
-            qb = n // H
-            return qb, (n % H) // GH, n % GH, n % H
+            return n // H, (n % H) // GH, n % GH, n % H
 
         def prepare_bank(live):
-            i = counters["tp"] % 2
+            i = counters["tp"] % N_TP
             counters["tp"] += 1
             for s in range(8):
                 if s in live:
@@ -115,11 +116,17 @@ def tile_flexattention_kernel(tc, qkv, out):
             return tps[i]
 
         def g_bias(g):
-            for h in range(GH * (g % 4), GH * (g % 4) + GH):
+            for h in range(GH * g, GH * g + GH):
                 sigma = 2.0 ** (-(h + 1) / 2.0) * math.sqrt(E)
-                nc.vector.tensor_scalar(
-                    out=bias_t[:, h], in0=dist_t[:], scalar1=-sigma, scalar2=None, op0=ALU.mult
-                )
+                if h >= GP_BIAS_FROM:
+                    nc.gpsimd.tensor_scalar(
+                        out=bias_t[:, h], in0=dist_t[:], scalar1=-sigma, scalar2=0.0,
+                        op0=ALU.mult, op1=ALU.add,
+                    )
+                else:
+                    nc.vector.tensor_scalar(
+                        out=bias_t[:, h], in0=dist_t[:], scalar1=-sigma, scalar2=None, op0=ALU.mult
+                    )
 
         def g_qk_transpose(g):
             qb, hg = g // 4, g % 4
@@ -155,11 +162,10 @@ def tile_flexattention_kernel(tc, qkv, out):
         def g_v_quantise(g):
             c, hg = g // 16, g % 4
             cols = slice(hg * GH * E, (hg + 1) * GH * E)
-            gv = st["gv", g]
             nc.vector.quantize_mx(
                 out=vcodes[:, c, cols].bitcast(FP8X4),
                 scales=vscales[:, c, cols],
-                in_=gv[:].rearrange("p x t -> p (x t)"),
+                in_=st["gv", g][:].rearrange("p x t -> p (x t)"),
             )
 
         def g_window_scores(g):
@@ -178,9 +184,15 @@ def tile_flexattention_kernel(tc, qkv, out):
                 )
             st["wb", g] = wb
 
-        def g_window_max(g):
+        def g_window_pass(g):
             mw = gsmall.tile([P, GH], F32, tag="mw", name="mw")
-            nc.vector.tensor_reduce(out=mw[:], in_=st["wb", g][:], axis=AX.X, op=ALU.max)
+            for j in range(GH):
+                z = zpool.tile([P, 5 * P], F32, tag="z", name="z")
+                nc.vector.tensor_scalar(
+                    out=z[:, 0:P], in0=st["wb", g][:, j, :], scalar1=-SCALE, scalar2=None,
+                    op0=ALU.mult, op1=ALU.min, accum_out=mw[:, j : j + 1],
+                )
+                st["z", GH * g + j] = z
             st["mw", g] = mw
 
         def g_mx(g):
@@ -210,18 +222,12 @@ def tile_flexattention_kernel(tc, qkv, out):
 
         def g_out(g):
             qb, hg = g // 4, g % 4
-            ob = st["ob", g]
-            rs = st["rs", g]
             rinv = gsmall.tile([P, GH], F32, tag="rinv", name="rinv")
-            if qb >= 4:
-                rt = gsmall.tile([P, GH], F32, tag="rt", name="rt")
-                nc.vector.tensor_reduce(out=rt[:], in_=rs[:], axis=AX.X, op=ALU.add)
-                nc.vector.reciprocal(out=rinv[:], in_=rt[:])
-            else:
-                nc.vector.reciprocal(out=rinv[:], in_=rs[:, :, 0])
+            nc.vector.reciprocal(out=rinv[:], in_=st["rs", g][:])
             ost = opool.tile([P, GH, P], F32, tag="ost", name="ost")
             nc.vector.tensor_tensor(
-                out=ost[:], in0=ob[:], in1=rinv[:].unsqueeze(2).to_broadcast([P, GH, P]), op=ALU.mult
+                out=ost[:], in0=st["ob", g][:], in1=rinv[:].unsqueeze(2).to_broadcast([P, GH, P]),
+                op=ALU.mult,
             )
             nc.sync.dma_start(out=out[0, qb * P : (qb + 1) * P, GH * hg : GH * hg + GH, :], in_=ost[:])
 
@@ -240,19 +246,21 @@ def tile_flexattention_kernel(tc, qkv, out):
             )
             st["sb", n] = sb
 
-        def t_max(n):
+        def t_pass(n):
             qb, hg, j, h = where(n)
             nb = min(qb + 1, 4)
-            m = small.tile([P, 1], F32, tag="m", name="m")
-            nc.vector.tensor_reduce(out=m[:], in_=st["sb", n][:, 0 : nb * P], axis=AX.X, op=ALU.max)
             nbias = small.tile([P, 1], F32, tag="nbias", name="nbias")
             if qb >= 4:
-                nc.vector.tensor_scalar(
-                    out=nbias[:], in0=m[:], scalar1=st["mw", n // GH][:, j : j + 1], scalar2=-SCALE,
-                    op0=ALU.max, op1=ALU.mult,
-                )
+                z = st["z", n]
+                first = st["mw", n // GH][:, j : j + 1]
             else:
-                nc.vector.tensor_scalar(out=nbias[:], in0=m[:], scalar1=-SCALE, scalar2=None, op0=ALU.mult)
+                z = zpool.tile([P, 5 * P], F32, tag="z", name="z")
+                st["z", n] = z
+                first = None
+            nc.vector.tensor_scalar(
+                out=z[:, P : P + nb * P], in0=st["sb", n][:, 0 : nb * P], scalar1=-SCALE, scalar2=first,
+                op0=ALU.mult, op1=ALU.min, accum_out=nbias[:],
+            )
             st["nbias", n] = nbias
 
         def t_exp(n):
@@ -260,20 +268,13 @@ def tile_flexattention_kernel(tc, qkv, out):
             nb = min(qb + 1, 4)
             g = n // GH
             if j == 0:
-                st["rs", g] = gsmall.tile([P, GH, 2], F32, tag="rs", name="rs")
-            rs = st["rs", g]
-            nbias = st["nbias", n]
-            sb = st["sb", n]
+                st["rs", g] = gsmall.tile([P, GH], F32, tag="rs", name="rs")
+            lo = 0 if qb >= 4 else P
             e = epool.tile([P, 5 * P], BF16, tag="e", name="e")
             nc.scalar.activation(
-                out=e[:, P : P + nb * P], in_=sb[:, 0 : nb * P], func=ACT.Exp,
-                bias=nbias[:], scale=SCALE, accum_out=rs[:, j, 0:1],
+                out=e[:, lo : P + nb * P], in_=st["z", n][:, lo : P + nb * P], func=ACT.Exp,
+                bias=st["nbias", n][:], scale=-1.0, accum_out=st["rs", g][:, j : j + 1],
             )
-            if qb >= 4:
-                nc.scalar.activation(
-                    out=e[:, 0:P], in_=st["wb", g][:, j, :], func=ACT.Exp,
-                    bias=nbias[:], scale=SCALE, accum_out=rs[:, j, 1:2],
-                )
             st["e", n] = e
 
         def t_transpose(n):
@@ -295,65 +296,80 @@ def tile_flexattention_kernel(tc, qkv, out):
 
         def t_copy(n):
             qb, hg, j, h = where(n)
-            bank = st["bank", n]
             if qb < 4 and j % 2 == 0:
                 return
             grp = gpool.tile([P, 2, P, 4], BF16, tag="grp", name="grp", align_bytes=64)
-            for c in range(2):
-                src = bank[:, 4 * c : 4 * c + 4, :].rearrange("p t q -> p q t")
-                if counters["evac"] % 8 in VEC_EVAC:
-                    nc.vector.tensor_copy(out=grp[:, c], in_=src)
-                else:
-                    nc.scalar.copy(out=grp[:, c], in_=src)
-                counters["evac"] += 1
+            src = st["bank", n][:].rearrange("p (c t) q -> p c q t", t=4)
+            if j in VEC_EVAC:
+                nc.vector.tensor_copy(out=grp[:], in_=src)
+            else:
+                nc.scalar.copy(out=grp[:], in_=src)
             st["grp", n] = grp
 
         def t_quantise(n):
             qb, hg, j, h = where(n)
             if qb < 4 and j % 2 == 0:
                 return
-            grp = st["grp", n]
             codes = cpool.tile([P, 2 * P], U32, tag="codes", name="codes", align_bytes=64)
             scl = cpool.tile([P, 2 * P], U8, tag="scl", name="scl", align_bytes=64)
             nc.vector.quantize_mx(
-                out=codes[:].bitcast(FP8X4), scales=scl[:], in_=grp[:].rearrange("p g q t -> p (g q t)")
+                out=codes[:].bitcast(FP8X4), scales=scl[:],
+                in_=st["grp", n][:].rearrange("p g q t -> p (g q t)"),
             )
             st["codes", n] = (codes, scl)
 
-        for s in range(-4, NT + 12):
-            g4, r4 = divmod(s + 4, 4)
-            if 0 <= s < NT:
-                t_scores(s)
-            if 0 <= s - 3 < NT:
-                t_transpose(s - 3)
-            if r4 == 0 and g4 < NG:
-                g_qk_transpose(g4)
-            if r4 == 3 and g4 < NG and g4 >= 16:
-                g_window_scores(g4)
-            gm = (s - 10) // 4
-            if (s - 10) % 4 == 0 and 0 <= gm < NG:
-                g_mx(gm)
-            if r4 == 1 and g4 < 4:
-                g_bias(g4)
-            if r4 == 1 and g4 < NG:
-                g_qk_copy(g4)
-            if s % 4 == 0 and 16 <= s // 4 < NG:
-                g_window_max(s // 4)
-            if 0 <= s - 1 < NT:
-                t_max(s - 1)
-            if 0 <= s - 2 < NT:
-                t_exp(s - 2)
-            if 0 <= s - 4 < NT:
-                t_copy(s - 4)
-            if 0 <= s - 5 < NT:
-                t_quantise(s - 5)
-            gv_g = (s - 2) // 4
-            if (s - 2) % 4 == 0 and 0 <= gv_g < NG and gv_g % 16 < 4:
-                g_v(gv_g)
-            if (s - 3) % 4 == 0 and 0 <= (s - 3) // 4 < NG and ((s - 3) // 4) % 16 < 4:
-                g_v_quantise((s - 3) // 4)
-            go = (s - 11) // 4
-            if (s - 11) % 4 == 0 and 0 <= go < NG:
-                g_out(go)
-            if s % H == 10 and 4 <= s // H + 4 < NQB:
-                load_x(s // H + 4)
+        def tile_at(s, lag):
+            return s - lag if 0 <= s - lag < NT else None
+
+        def group_at(s, off, lo=0, hi=NG):
+            g, r = divmod(s - off, GH)
+            return g if r == 0 and lo <= g < hi else None
+
+        for s in range(G_QKT, NT + G_OUT):
+            n = tile_at(s, 0)
+            if n is not None:
+                t_scores(n)
+            n = tile_at(s, LAG_TR)
+            if n is not None:
+                t_transpose(n)
+            g = group_at(s, G_QKT)
+            if g is not None:
+                g_qk_transpose(g)
+            g = group_at(s, G_W, lo=16)
+            if g is not None:
+                g_window_scores(g)
+            g = group_at(s, G_MX)
+            if g is not None:
+                g_mx(g)
+            g = group_at(s, G_BIAS, hi=4)
+            if g is not None:
+                g_bias(g)
+            g = group_at(s, G_QKCOPY)
+            if g is not None:
+                g_qk_copy(g)
+            g = group_at(s, G_WPASS, lo=16)
+            if g is not None:
+                g_window_pass(g)
+            n = tile_at(s, LAG_PASS)
+            if n is not None:
+                t_pass(n)
+            n = tile_at(s, LAG_EXP)
+            if n is not None:
+                t_exp(n)
+            n = tile_at(s, LAG_COPY)
+            if n is not None:
+                t_copy(n)
+            n = tile_at(s, LAG_Q)
+            if n is not None:
+                t_quantise(n)
+            g = group_at(s, G_V)
+            if g is not None and g % 16 < 4:
+                g_v(g)
+            g = group_at(s, G_VQ)
+            if g is not None and g % 16 < 4:
+                g_v_quantise(g)
+            g = group_at(s, G_OUT)
+            if g is not None:
+                g_out(g)
+            if s % H == 10 and N_X <= s // H + N_X < NQB:
+                load_x(s // H + N_X)

@@ -26,7 +26,9 @@ FLOPS = 4 * E * H * (512 * 512 + 512 * 1024)
 
 N_TP = 3
 N_X = 3
-VEC_EVAC = (1,)
+VEC_HALVES = (1, 4, 7)
+VEC_PAIRS = (1,)
+N_GRP = 4
 GP_BIAS_FROM = 4
 LAG_PASS, LAG_EXP, LAG_TR, LAG_COPY, LAG_Q = 1, 2, 4, 5, 7
 G_QKT, G_QKCOPY, G_BIAS, G_W, G_WPASS, G_V, G_VQ, G_MX, G_OUT = -4, -3, -3, -2, 0, 2, 4, 14, 15
@@ -44,7 +46,6 @@ def tile_flexattention_kernel(tc, qkv, out):
         gsmall = ctx.enter_context(tc.tile_pool(name="gsmall", bufs=7))
         zpool = ctx.enter_context(tc.tile_pool(name="zpool", bufs=8))
         epool = ctx.enter_context(tc.tile_pool(name="epool", bufs=4))
-        gpool = ctx.enter_context(tc.tile_pool(name="gpool", bufs=4))
         cpool = ctx.enter_context(tc.tile_pool(name="cpool", bufs=12))
         opool = ctx.enter_context(tc.tile_pool(name="opool", bufs=3))
         ps_s = ctx.enter_context(tc.psum_pool(name="ps_s", bufs=3))
@@ -90,30 +91,25 @@ def tile_flexattention_kernel(tc, qkv, out):
         )
         ident_f = const.tile([P, P], F32, name="ident_f")
         make_identity(nc, ident_f[:])
-        zero_bf = const.tile([P, P], BF16, name="zero_bf")
-        nc.vector.memset(zero_bf[:], 0.0)
         bias_t = const.tile([P, H, 5, P], F32, name="bias_t")
         k_t = const.tile([P, H, L], BF16, name="k_t")
         vcodes = const.tile([P, 2, H * E], U32, name="vcodes", align_bytes=64)
         vscales = const.tile([P, 2, H * E], U8, name="vscales", align_bytes=64)
         tps = [ps_t.tile([P, 8, P], BF16, name="tp%d" % i) for i in range(N_TP)]
-        tp_zero = [[False] * 8 for i in range(N_TP)]
-        counters = {"tp": 0}
+        grp_lo = [const.tile([P, 2, P, 4], BF16, name="grp_lo%d" % i, align_bytes=64) for i in range(N_GRP)]
+        grp_up = [const.tile([P, 2, P, 4], BF16, name="grp_up%d" % i, align_bytes=64) for i in range(N_GRP)]
+        for t in grp_lo:
+            nc.vector.memset(t[:], 0.0)
+        grp_qb = [4] * N_GRP
+        counters = {"tp": 0, "grp": 0}
         st = {}
 
         def where(n):
             return n // H, (n % H) // GH, n % GH, n % H
 
-        def prepare_bank(live):
-            i = counters["tp"] % N_TP
+        def next_bank():
             counters["tp"] += 1
-            for s in range(8):
-                if s in live:
-                    tp_zero[i][s] = False
-                elif not tp_zero[i][s]:
-                    nc.tensor.transpose(tps[i][:, s, :], zero_bf[:], ident_bf[:])
-                    tp_zero[i][s] = True
-            return tps[i]
+            return tps[counters["tp"] % N_TP]
 
         def g_bias(g):
             for h in range(GH * g, GH * g + GH):
@@ -127,6 +123,10 @@ def tile_flexattention_kernel(tc, qkv, out):
                     nc.vector.tensor_scalar(
                         out=bias_t[:, h], in0=dist_t[:], scalar1=-sigma, scalar2=None, op0=ALU.mult
                     )
+
+        def g_zero_upper():
+            for t in grp_up:
+                nc.gpsimd.memset(t[:], 0.0)
 
         def g_qk_transpose(g):
             qb, hg = g // 4, g % 4
@@ -282,12 +282,12 @@ def tile_flexattention_kernel(tc, qkv, out):
             nb = min(qb + 1, 4)
             e = st["e", n]
             if qb >= 4:
-                bank = prepare_bank(set(range(qb - 4, qb + 1)))
+                bank = next_bank()
                 nc.tensor.transpose(bank[:, qb - 4, :], e[:, 0:P], ident_bf[:])
                 first = qb - 3
             else:
                 if j % 2 == 0:
-                    st["pair_bank"] = prepare_bank(set(range(nb)) | set(range(4, 4 + nb)))
+                    st["pair_bank"] = next_bank()
                 bank = st["pair_bank"]
                 first = 4 * (j % 2)
             for b in range(nb):
@@ -298,12 +298,28 @@ def tile_flexattention_kernel(tc, qkv, out):
             qb, hg, j, h = where(n)
             if qb < 4 and j % 2 == 0:
                 return
-            grp = gpool.tile([P, 2, P, 4], BF16, tag="grp", name="grp", align_bytes=64)
-            src = st["bank", n][:].rearrange("p (c t) q -> p c q t", t=4)
-            if j in VEC_EVAC:
-                nc.vector.tensor_copy(out=grp[:], in_=src)
+            counters["grp"] += 1
+            i = counters["grp"] % N_GRP
+            bank = st["bank", n]
+            if qb < 4:
+                nb = qb + 1
+                grp = grp_lo[i]
+                src = bank[:].rearrange("p (c t) q -> p c q t", t=4)[:, :, :, 0:nb]
+                if j in VEC_PAIRS:
+                    nc.vector.tensor_copy(out=grp[:, :, :, 0:nb], in_=src)
+                else:
+                    nc.scalar.copy(out=grp[:, :, :, 0:nb], in_=src)
             else:
-                nc.scalar.copy(out=grp[:], in_=src)
+                grp = grp_up[i]
+                if grp_qb[i] != qb:
+                    nc.vector.memset(grp[:, 0], 0.0)
+                    grp_qb[i] = qb
+                for c, (lo, hi) in enumerate(((qb - 4, 4), (0, qb - 3))):
+                    src = bank[:, 4 * c + lo : 4 * c + hi, :].rearrange("p t q -> p q t")
+                    if 2 * j + c in VEC_HALVES:
+                        nc.vector.tensor_copy(out=grp[:, c, :, lo:hi], in_=src)
+                    else:
+                        nc.scalar.copy(out=grp[:, c, :, lo:hi], in_=src)
             st["grp", n] = grp
 
         def t_quantise(n):
@@ -344,6 +360,8 @@ def tile_flexattention_kernel(tc, qkv, out):
             g = group_at(s, G_BIAS, hi=4)
             if g is not None:
                 g_bias(g)
+                if g == 3:
+                    g_zero_upper()
             g = group_at(s, G_QKCOPY)
             if g is not None:
                 g_qk_copy(g)

@@ -26,12 +26,10 @@ FLOPS = 4 * E * H * (512 * 512 + 512 * 1024)
 
 N_TP = 3
 N_X = 3
-VEC_HALVES = (1, 4, 7)
-VEC_PAIRS = (1,)
-N_GRP = 4
+VEC_EVAC = (1,)
 GP_BIAS_FROM = 4
-LAG_PASS, LAG_EXP, LAG_TR, LAG_COPY, LAG_Q = 1, 2, 4, 5, 7
-G_QKT, G_QKCOPY, G_BIAS, G_W, G_WPASS, G_V, G_VQ, G_MX, G_OUT = -4, -3, -3, -2, 0, 2, 4, 14, 15
+LAG_PASS, LAG_EXP, LAG_TR, LAG_COPY, LAG_Q = 1, 3, 5, 6, 8
+G_QKT, G_QKCOPY, G_BIAS, G_W, G_WPASS, G_V, G_VQ, G_MX, G_OUT = -8, -6, -6, -1, 0, 2, 4, 17, 18
 
 
 def tile_flexattention_kernel(tc, qkv, out):
@@ -40,18 +38,18 @@ def tile_flexattention_kernel(tc, qkv, out):
         ctx.enter_context(tc.manual_schedule())
         const = ctx.enter_context(tc.tile_pool(name="const", bufs=1))
         ld = ctx.enter_context(tc.tile_pool(name="ld", bufs=N_X))
-        qpool = ctx.enter_context(tc.tile_pool(name="qpool", bufs=3))
+        qpool = ctx.enter_context(tc.tile_pool(name="qpool", bufs=4))
         vpool = ctx.enter_context(tc.tile_pool(name="vpool", bufs=2))
         small = ctx.enter_context(tc.tile_pool(name="small", bufs=8))
         gsmall = ctx.enter_context(tc.tile_pool(name="gsmall", bufs=7))
         zpool = ctx.enter_context(tc.tile_pool(name="zpool", bufs=8))
         epool = ctx.enter_context(tc.tile_pool(name="epool", bufs=4))
+        gpool = ctx.enter_context(tc.tile_pool(name="gpool", bufs=4))
         cpool = ctx.enter_context(tc.tile_pool(name="cpool", bufs=12))
         opool = ctx.enter_context(tc.tile_pool(name="opool", bufs=3))
         ps_s = ctx.enter_context(tc.psum_pool(name="ps_s", bufs=3))
-        ps_w = ctx.enter_context(tc.psum_pool(name="ps_w", bufs=1))
         ps_t = ctx.enter_context(tc.psum_pool(name="ps_t", bufs=1))
-        ps_x = ctx.enter_context(tc.psum_pool(name="ps_x", bufs=1))
+        ps_a = ctx.enter_context(tc.psum_pool(name="ps_a", bufs=2))
 
         xs = {}
         vraw = const.tile([P, NQB, H * E], BF16, name="vraw")
@@ -91,25 +89,30 @@ def tile_flexattention_kernel(tc, qkv, out):
         )
         ident_f = const.tile([P, P], F32, name="ident_f")
         make_identity(nc, ident_f[:])
+        zero_bf = const.tile([P, P], BF16, name="zero_bf")
+        nc.vector.memset(zero_bf[:], 0.0)
         bias_t = const.tile([P, H, 5, P], F32, name="bias_t")
         k_t = const.tile([P, H, L], BF16, name="k_t")
         vcodes = const.tile([P, 2, H * E], U32, name="vcodes", align_bytes=64)
         vscales = const.tile([P, 2, H * E], U8, name="vscales", align_bytes=64)
         tps = [ps_t.tile([P, 8, P], BF16, name="tp%d" % i) for i in range(N_TP)]
-        grp_lo = [const.tile([P, 2, P, 4], BF16, name="grp_lo%d" % i, align_bytes=64) for i in range(N_GRP)]
-        grp_up = [const.tile([P, 2, P, 4], BF16, name="grp_up%d" % i, align_bytes=64) for i in range(N_GRP)]
-        for t in grp_lo:
-            nc.vector.memset(t[:], 0.0)
-        grp_qb = [4] * N_GRP
-        counters = {"tp": 0, "grp": 0}
+        tp_zero = [[False] * 8 for i in range(N_TP)]
+        counters = {"tp": 0}
         st = {}
 
         def where(n):
             return n // H, (n % H) // GH, n % GH, n % H
 
-        def next_bank():
+        def prepare_bank(live):
+            i = counters["tp"] % N_TP
             counters["tp"] += 1
-            return tps[counters["tp"] % N_TP]
+            for s in range(8):
+                if s in live:
+                    tp_zero[i][s] = False
+                elif not tp_zero[i][s]:
+                    nc.tensor.transpose(tps[i][:, s, :], zero_bf[:], ident_bf[:])
+                    tp_zero[i][s] = True
+            return tps[i]
 
         def g_bias(g):
             for h in range(GH * g, GH * g + GH):
@@ -124,13 +127,9 @@ def tile_flexattention_kernel(tc, qkv, out):
                         out=bias_t[:, h], in0=dist_t[:], scalar1=-sigma, scalar2=None, op0=ALU.mult
                     )
 
-        def g_zero_upper():
-            for t in grp_up:
-                nc.gpsimd.memset(t[:], 0.0)
-
         def g_qk_transpose(g):
             qb, hg = g // 4, g % 4
-            qk_ps = ps_x.tile([P, 8, P], BF16, tag="x", name="qk_ps")
+            qk_ps = ps_a.tile([P, 8, P], BF16, tag="a", name="qk_ps")
             for j in range(GH):
                 h = GH * hg + j
                 nc.tensor.transpose(qk_ps[:, j, :], xs[qb][:, h * E : (h + 1) * E], ident_bf[:])
@@ -170,7 +169,7 @@ def tile_flexattention_kernel(tc, qkv, out):
 
         def g_window_scores(g):
             qb, hg = g // 4, g % 4
-            wb = ps_w.tile([P, GH, P], F32, tag="w", name="wb")
+            wb = ps_a.tile([P, GH, P], F32, tag="a", name="wb")
             q_t = st["q_t", g]
             for j in range(GH):
                 h = GH * hg + j
@@ -197,7 +196,7 @@ def tile_flexattention_kernel(tc, qkv, out):
 
         def g_mx(g):
             qb, hg = g // 4, g % 4
-            ob = ps_x.tile([P, GH, P], F32, tag="x", name="ob")
+            ob = ps_a.tile([P, GH, P], F32, tag="a", name="ob")
             for j in range(GH):
                 h = GH * hg + j
                 fcols = slice(h * E, (h + 1) * E)
@@ -282,12 +281,12 @@ def tile_flexattention_kernel(tc, qkv, out):
             nb = min(qb + 1, 4)
             e = st["e", n]
             if qb >= 4:
-                bank = next_bank()
+                bank = prepare_bank(set(range(qb - 4, qb + 1)))
                 nc.tensor.transpose(bank[:, qb - 4, :], e[:, 0:P], ident_bf[:])
                 first = qb - 3
             else:
                 if j % 2 == 0:
-                    st["pair_bank"] = next_bank()
+                    st["pair_bank"] = prepare_bank(set(range(nb)) | set(range(4, 4 + nb)))
                 bank = st["pair_bank"]
                 first = 4 * (j % 2)
             for b in range(nb):
@@ -298,28 +297,12 @@ def tile_flexattention_kernel(tc, qkv, out):
             qb, hg, j, h = where(n)
             if qb < 4 and j % 2 == 0:
                 return
-            counters["grp"] += 1
-            i = counters["grp"] % N_GRP
-            bank = st["bank", n]
-            if qb < 4:
-                nb = qb + 1
-                grp = grp_lo[i]
-                src = bank[:].rearrange("p (c t) q -> p c q t", t=4)[:, :, :, 0:nb]
-                if j in VEC_PAIRS:
-                    nc.vector.tensor_copy(out=grp[:, :, :, 0:nb], in_=src)
-                else:
-                    nc.scalar.copy(out=grp[:, :, :, 0:nb], in_=src)
+            grp = gpool.tile([P, 2, P, 4], BF16, tag="grp", name="grp", align_bytes=64)
+            src = st["bank", n][:].rearrange("p (c t) q -> p c q t", t=4)
+            if j in VEC_EVAC:
+                nc.vector.tensor_copy(out=grp[:], in_=src)
             else:
-                grp = grp_up[i]
-                if grp_qb[i] != qb:
-                    nc.vector.memset(grp[:, 0], 0.0)
-                    grp_qb[i] = qb
-                for c, (lo, hi) in enumerate(((qb - 4, 4), (0, qb - 3))):
-                    src = bank[:, 4 * c + lo : 4 * c + hi, :].rearrange("p t q -> p q t")
-                    if 2 * j + c in VEC_HALVES:
-                        nc.vector.tensor_copy(out=grp[:, c, :, lo:hi], in_=src)
-                    else:
-                        nc.scalar.copy(out=grp[:, c, :, lo:hi], in_=src)
+                nc.scalar.copy(out=grp[:], in_=src)
             st["grp", n] = grp
 
         def t_quantise(n):
@@ -360,8 +343,6 @@ def tile_flexattention_kernel(tc, qkv, out):
             g = group_at(s, G_BIAS, hi=4)
             if g is not None:
                 g_bias(g)
-                if g == 3:
-                    g_zero_upper()
             g = group_at(s, G_QKCOPY)
             if g is not None:
                 g_qk_copy(g)
@@ -389,5 +370,5 @@ def tile_flexattention_kernel(tc, qkv, out):
             g = group_at(s, G_OUT)
             if g is not None:
                 g_out(g)
-            if s % H == 10 and N_X <= s // H + N_X < NQB:
+            if s % H == 6 and N_X <= s // H + N_X < NQB:
                 load_x(s // H + N_X)

@@ -26,7 +26,7 @@ FLOPS = 4 * E * H * (512 * 512 + 512 * 1024)
 
 N_TP = 3
 N_X = 3
-VEC_EVAC = (1,)
+VEC_BANKS = (0, 0, 0, 2, 1, 5, 4, 4)
 GP_BIAS_FROM = 4
 LAG_PASS, LAG_EXP, LAG_TR, LAG_COPY, LAG_Q = 1, 3, 5, 6, 8
 G_QKT, G_QKCOPY, G_BIAS, G_W, G_WPASS, G_V, G_VQ, G_MX, G_OUT = -8, -6, -6, -1, 0, 2, 4, 17, 18
@@ -299,7 +299,8 @@ def tile_flexattention_kernel(tc, qkv, out):
                 return
             grp = gpool.tile([P, 2, P, 4], BF16, tag="grp", name="grp", align_bytes=64)
             src = st["bank", n][:].rearrange("p (c t) q -> p c q t", t=4)
-            if j in VEC_EVAC:
+            units, u = (8, h // 2) if qb < 4 else (16, h)
+            if (u + 1) * VEC_BANKS[qb] // units > u * VEC_BANKS[qb] // units:
                 nc.vector.tensor_copy(out=grp[:], in_=src)
             else:
                 nc.scalar.copy(out=grp[:], in_=src)

@@ -26,7 +26,7 @@ FLOPS = 4 * E * H * (512 * 512 + 512 * 1024)
 
 N_TP = 3
 N_X = 3
-VEC_BANKS = (0, 0, 0, 2, 1, 5, 4, 4)
+VEC_BANKS = (0, 0, 0, 2, 1, 4, 4, 4)
 GP_BIAS_FROM = 4
 LAG_PASS, LAG_EXP, LAG_TR, LAG_COPY, LAG_Q = 1, 3, 5, 6, 8
 G_QKT, G_QKCOPY, G_BIAS, G_W, G_WPASS, G_V, G_VQ, G_MX, G_OUT = -8, -6, -6, -1, 0, 2, 4, 17, 18
@@ -55,15 +55,17 @@ def tile_flexattention_kernel(tc, qkv, out):
         vraw = const.tile([P, NQB, H * E], BF16, name="vraw")
         vsrc = qkv[0, :, 2].rearrange("(k p) h e -> p k (h e)", p=P)
 
-        def load_x(pb):
-            x = ld.tile([P, 2 * H * E], BF16, tag="x", name="x")
-            nc.sync.dma_start(
-                out=x[:],
-                in_=qkv[0, pb * P : (pb + 1) * P, 0:2].rearrange("p w h e -> p (w h e)"),
-            )
+        def load_x(pb, pieces=1):
+            x = ld.tile([P, 2, H * E], BF16, tag="x", name="x")
+            src = qkv[0, pb * P : (pb + 1) * P, 0:2].rearrange("p w h e -> p w (h e)")
+            width = H * E // pieces
+            for i in range(pieces):
+                nc.sync.dma_start(
+                    out=x[:, :, i * width : (i + 1) * width], in_=src[:, :, i * width : (i + 1) * width]
+                )
             xs[pb] = x
 
-        load_x(0)
+        load_x(0, pieces=H // GH)
         nc.sync.dma_start(out=vraw[:, 0:4, :], in_=vsrc[:, 0:4, :])
         for pb in range(1, N_X):
             load_x(pb)
@@ -132,9 +134,9 @@ def tile_flexattention_kernel(tc, qkv, out):
             qk_ps = ps_a.tile([P, 8, P], BF16, tag="a", name="qk_ps")
             for j in range(GH):
                 h = GH * hg + j
-                nc.tensor.transpose(qk_ps[:, j, :], xs[qb][:, h * E : (h + 1) * E], ident_bf[:])
+                nc.tensor.transpose(qk_ps[:, j, :], xs[qb][:, 0, h * E : (h + 1) * E], ident_bf[:])
                 nc.tensor.transpose(
-                    qk_ps[:, GH + j, :], xs[qb][:, (H + h) * E : (H + h + 1) * E], ident_bf[:]
+                    qk_ps[:, GH + j, :], xs[qb][:, 1, h * E : (h + 1) * E], ident_bf[:]
                 )
             st["qk_ps", g] = qk_ps
 

@@ -26,7 +26,7 @@ FLOPS = 4 * E * H * (512 * 512 + 512 * 1024)
 
 N_TP = 3
 N_X = 3
-VEC_BANKS = (0, 0, 0, 2, 1, 4, 4, 4)
+VEC_BANKS = (0, 0, 0, 0, 0, 2, 2, 2)
 GP_BIAS_FROM = 4
 LAG_PASS, LAG_EXP, LAG_TR, LAG_COPY, LAG_Q = 1, 3, 5, 6, 8
 G_QKT, G_QKCOPY, G_BIAS, G_W, G_WPASS, G_V, G_VQ, G_MX, G_OUT = -8, -6, -6, -1, 0, 2, 4, 17, 18

@@ -26,7 +26,7 @@ FLOPS = 4 * E * H * (512 * 512 + 512 * 1024)
 
 N_TP = 3
 N_X = 3
-VEC_BANKS = (0, 0, 0, 0, 0, 2, 2, 2)
+VEC_BANKS = (1, 2, 2, 2, 1, 4, 4, 4)
 GP_BIAS_FROM = 4
 LAG_PASS, LAG_EXP, LAG_TR, LAG_COPY, LAG_Q = 1, 3, 5, 6, 8
 G_QKT, G_QKCOPY, G_BIAS, G_W, G_WPASS, G_V, G_VQ, G_MX, G_OUT = -8, -6, -6, -1, 0, 2, 4, 17, 18

from contextlib import ExitStack
import math

import concourse.mybir as mybir
from concourse.masks import make_identity

F32 = mybir.dt.float32
BF16 = mybir.dt.bfloat16
U32 = mybir.dt.uint32
U8 = mybir.dt.uint8
FP8X4 = mybir.dt.float8_e4m3fn_x4
ALU = mybir.AluOpType
ACT = mybir.ActivationFunctionType

P = 128
H = 16
L = 1024
E = 128
NQB = L // P
GH = 4
NG = NQB * H // GH
NT = NQB * H
SCALE = 1.0 / math.sqrt(E)
MASKED = 1.0e30
FLOPS = 4 * E * H * (512 * 512 + 512 * 1024)

N_TP = 3
N_X = 3
VEC_BANKS = (1, 2, 2, 2, 1, 4, 4, 4)
GP_BIAS_FROM = 4
LAG_PASS, LAG_EXP, LAG_TR, LAG_COPY, LAG_Q = 1, 3, 5, 6, 8
G_QKT, G_QKCOPY, G_BIAS, G_W, G_WPASS, G_V, G_VQ, G_MX, G_OUT = -8, -6, -6, -1, 0, 2, 4, 17, 18


def tile_flexattention_kernel(tc, qkv, out):
    nc = tc.nc
    with ExitStack() as ctx:
        ctx.enter_context(tc.manual_schedule())
        const = ctx.enter_context(tc.tile_pool(name="const", bufs=1))
        ld = ctx.enter_context(tc.tile_pool(name="ld", bufs=N_X))
        qpool = ctx.enter_context(tc.tile_pool(name="qpool", bufs=4))
        vpool = ctx.enter_context(tc.tile_pool(name="vpool", bufs=2))
        small = ctx.enter_context(tc.tile_pool(name="small", bufs=8))
        gsmall = ctx.enter_context(tc.tile_pool(name="gsmall", bufs=7))
        zpool = ctx.enter_context(tc.tile_pool(name="zpool", bufs=8))
        epool = ctx.enter_context(tc.tile_pool(name="epool", bufs=4))
        gpool = ctx.enter_context(tc.tile_pool(name="gpool", bufs=4))
        cpool = ctx.enter_context(tc.tile_pool(name="cpool", bufs=12))
        opool = ctx.enter_context(tc.tile_pool(name="opool", bufs=3))
        ps_s = ctx.enter_context(tc.psum_pool(name="ps_s", bufs=3))
        ps_t = ctx.enter_context(tc.psum_pool(name="ps_t", bufs=1))
        ps_a = ctx.enter_context(tc.psum_pool(name="ps_a", bufs=2))

        xs = {}
        vraw = const.tile([P, NQB, H * E], BF16, name="vraw")
        vsrc = qkv[0, :, 2].rearrange("(k p) h e -> p k (h e)", p=P)

        def load_x(pb, pieces=1):
            x = ld.tile([P, 2, H * E], BF16, tag="x", name="x")
            src = qkv[0, pb * P : (pb + 1) * P, 0:2].rearrange("p w h e -> p w (h e)")
            width = H * E // pieces
            for i in range(pieces):
                nc.sync.dma_start(
                    out=x[:, :, i * width : (i + 1) * width], in_=src[:, :, i * width : (i + 1) * width]
                )
            xs[pb] = x

        load_x(0, pieces=H // GH)
        nc.sync.dma_start(out=vraw[:, 0:4, :], in_=vsrc[:, 0:4, :])
        for pb in range(1, N_X):
            load_x(pb)
        nc.sync.dma_start(out=vraw[:, 4:8, :], in_=vsrc[:, 4:8, :])

        ident_bf = const.tile([P, P], BF16, name="ident_bf")
        make_identity(nc, ident_bf[:])
        dist_t = const.tile([P, 5, P], F32, name="dist_t")
        nc.gpsimd.iota(
            dist_t[:],
            pattern=[[P, 5], [1, P]],
            base=0,
            channel_multiplier=-1,
            allow_small_or_imprecise_dtypes=True,
        )
        nc.gpsimd.affine_select(
            out=dist_t[:, 0, :], in_=dist_t[:, 0, :], pattern=[[1, P]],
            compare_op=ALU.is_ge, fill=MASKED, base=0, channel_multiplier=-1,
        )
        nc.gpsimd.affine_select(
            out=dist_t[:, 4, :], in_=dist_t[:, 4, :], pattern=[[-1, P]],
            compare_op=ALU.is_gt, fill=MASKED, base=0, channel_multiplier=1,
        )
        ident_f = const.tile([P, P], F32, name="ident_f")
        make_identity(nc, ident_f[:])
        zero_bf = const.tile([P, P], BF16, name="zero_bf")
        nc.vector.memset(zero_bf[:], 0.0)
        bias_t = const.tile([P, H, 5, P], F32, name="bias_t")
        k_t = const.tile([P, H, L], BF16, name="k_t")
        vcodes = const.tile([P, 2, H * E], U32, name="vcodes", align_bytes=64)
        vscales = const.tile([P, 2, H * E], U8, name="vscales", align_bytes=64)
        tps = [ps_t.tile([P, 8, P], BF16, name="tp%d" % i) for i in range(N_TP)]
        tp_zero = [[False] * 8 for i in range(N_TP)]
        counters = {"tp": 0}
        st = {}

        def where(n):
            return n // H, (n % H) // GH, n % GH, n % H

        def prepare_bank(live):
            i = counters["tp"] % N_TP
            counters["tp"] += 1
            for s in range(8):
                if s in live:
                    tp_zero[i][s] = False
                elif not tp_zero[i][s]:
                    nc.tensor.transpose(tps[i][:, s, :], zero_bf[:], ident_bf[:])
                    tp_zero[i][s] = True
            return tps[i]

        def g_bias(g):
            for h in range(GH * g, GH * g + GH):
                sigma = 2.0 ** (-(h + 1) / 2.0) * math.sqrt(E)
                if h >= GP_BIAS_FROM:
                    nc.gpsimd.tensor_scalar(
                        out=bias_t[:, h], in0=dist_t[:], scalar1=-sigma, scalar2=0.0,
                        op0=ALU.mult, op1=ALU.add,
                    )
                else:
                    nc.vector.tensor_scalar(
                        out=bias_t[:, h], in0=dist_t[:], scalar1=-sigma, scalar2=None, op0=ALU.mult
                    )

        def g_qk_transpose(g):
            qb, hg = g // 4, g % 4
            qk_ps = ps_a.tile([P, 8, P], BF16, tag="a", name="qk_ps")
            for j in range(GH):
                h = GH * hg + j
                nc.tensor.transpose(qk_ps[:, j, :], xs[qb][:, 0, h * E : (h + 1) * E], ident_bf[:])
                nc.tensor.transpose(
                    qk_ps[:, GH + j, :], xs[qb][:, 1, h * E : (h + 1) * E], ident_bf[:]
                )
            st["qk_ps", g] = qk_ps

        def g_qk_copy(g):
            qb, hg = g // 4, g % 4
            qk_ps = st["qk_ps", g]
            q_t = qpool.tile([P, GH, P], BF16, tag="q_t", name="q_t")
            nc.scalar.copy(out=q_t[:], in_=qk_ps[:, 0:GH, :])
            nc.scalar.copy(
                out=k_t[:, GH * hg : GH * hg + GH, qb * P : (qb + 1) * P], in_=qk_ps[:, GH : 2 * GH, :]
            )
            st["q_t", g] = q_t

        def g_v(g):
            c, hg = g // 16, g % 4
            cols = slice(hg * GH * E, (hg + 1) * GH * E)
            gv = vpool.tile([P, GH * E, 4], BF16, tag="gv", name="gv", align_bytes=64)
            nc.vector.tensor_copy(
                out=gv[:].rearrange("p (c i) t -> p c t i", i=4),
                in_=vraw[:, 4 * c : 4 * c + 4, cols].rearrange("p t (c i) -> p c t i", i=4),
            )
            st["gv", g] = gv

        def g_v_quantise(g):
            c, hg = g // 16, g % 4
            cols = slice(hg * GH * E, (hg + 1) * GH * E)
            nc.vector.quantize_mx(
                out=vcodes[:, c, cols].bitcast(FP8X4),
                scales=vscales[:, c, cols],
                in_=st["gv", g][:].rearrange("p x t -> p (x t)"),
            )

        def g_window_scores(g):
            qb, hg = g // 4, g % 4
            wb = ps_a.tile([P, GH, P], F32, tag="a", name="wb")
            q_t = st["q_t", g]
            for j in range(GH):
                h = GH * hg + j
                nc.tensor.matmul(
                    wb[:, j, :], lhsT=bias_t[:, h, 4, :], rhs=ident_f[:],
                    is_transpose=True, start=True, stop=False,
                )
                nc.tensor.matmul(
                    wb[:, j, :], lhsT=q_t[:, j, :], rhs=k_t[:, h, (qb - 4) * P : (qb - 3) * P],
                    start=False, stop=True,
                )
            st["wb", g] = wb

        def g_window_pass(g):
            mw = gsmall.tile([P, GH], F32, tag="mw", name="mw")
            for j in range(GH):
                z = zpool.tile([P, 5 * P], F32, tag="z", name="z")
                nc.vector.tensor_scalar(
                    out=z[:, 0:P], in0=st["wb", g][:, j, :], scalar1=-SCALE, scalar2=None,
                    op0=ALU.mult, op1=ALU.min, accum_out=mw[:, j : j + 1],
                )
                st["z", GH * g + j] = z
            st["mw", g] = mw

        def g_mx(g):
            qb, hg = g // 4, g % 4
            ob = ps_a.tile([P, GH, P], F32, tag="a", name="ob")
            for j in range(GH):
                h = GH * hg + j
                fcols = slice(h * E, (h + 1) * E)
                if qb >= 4:
                    codes, scl = st["codes", GH * g + j]
                    passes = [(0, 0), (1, 1)]
                else:
                    codes, scl = st["codes", GH * g + (j // 2) * 2 + 1]
                    passes = [(j % 2, 0)]
                for i, (half, c) in enumerate(passes):
                    qcols = slice(half * P, (half + 1) * P)
                    nc.tensor.matmul_mx(
                        out=ob[:, j, :],
                        lhsT=codes[:, qcols].bitcast(FP8X4),
                        lhsT_scale=scl[:, qcols],
                        rhs=vcodes[:, c, fcols].bitcast(FP8X4),
                        rhs_scale=vscales[:, c, fcols],
                        start=(i == 0),
                        stop=(i == len(passes) - 1),
                    )
            st["ob", g] = ob

        def g_out(g):
            qb, hg = g // 4, g % 4
            rinv = gsmall.tile([P, GH], F32, tag="rinv", name="rinv")
            nc.vector.reciprocal(out=rinv[:], in_=st["rs", g][:])
            ost = opool.tile([P, GH, P], F32, tag="ost", name="ost")
            nc.vector.tensor_tensor(
                out=ost[:], in0=st["ob", g][:], in1=rinv[:].unsqueeze(2).to_broadcast([P, GH, P]),
                op=ALU.mult,
            )
            nc.sync.dma_start(out=out[0, qb * P : (qb + 1) * P, GH * hg : GH * hg + GH, :], in_=ost[:])

        def t_scores(n):
            qb, hg, j, h = where(n)
            nb = min(qb + 1, 4)
            sb = ps_s.tile([P, 4 * P], F32, tag="s", name="sb")
            for b in range(nb):
                nc.tensor.matmul(
                    sb[:, b * P : (b + 1) * P], lhsT=bias_t[:, h, nb - 1 - b, :], rhs=ident_f[:],
                    is_transpose=True, start=(b == 0), stop=False,
                )
            nc.tensor.matmul(
                sb[:, 0 : nb * P], lhsT=st["q_t", n // GH][:, j, :],
                rhs=k_t[:, h, (qb - nb + 1) * P : (qb + 1) * P], start=False, stop=True,
            )
            st["sb", n] = sb

        def t_pass(n):
            qb, hg, j, h = where(n)
            nb = min(qb + 1, 4)
            nbias = small.tile([P, 1], F32, tag="nbias", name="nbias")
            if qb >= 4:
                z = st["z", n]
                first = st["mw", n // GH][:, j : j + 1]
            else:
                z = zpool.tile([P, 5 * P], F32, tag="z", name="z")
                st["z", n] = z
                first = None
            nc.vector.tensor_scalar(
                out=z[:, P : P + nb * P], in0=st["sb", n][:, 0 : nb * P], scalar1=-SCALE, scalar2=first,
                op0=ALU.mult, op1=ALU.min, accum_out=nbias[:],
            )
            st["nbias", n] = nbias

        def t_exp(n):
            qb, hg, j, h = where(n)
            nb = min(qb + 1, 4)
            g = n // GH
            if j == 0:
                st["rs", g] = gsmall.tile([P, GH], F32, tag="rs", name="rs")
            lo = 0 if qb >= 4 else P
            e = epool.tile([P, 5 * P], BF16, tag="e", name="e")
            nc.scalar.activation(
                out=e[:, lo : P + nb * P], in_=st["z", n][:, lo : P + nb * P], func=ACT.Exp,
                bias=st["nbias", n][:], scale=-1.0, accum_out=st["rs", g][:, j : j + 1],
            )
            st["e", n] = e

        def t_transpose(n):
            qb, hg, j, h = where(n)
            nb = min(qb + 1, 4)
            e = st["e", n]
            if qb >= 4:
                bank = prepare_bank(set(range(qb - 4, qb + 1)))
                nc.tensor.transpose(bank[:, qb - 4, :], e[:, 0:P], ident_bf[:])
                first = qb - 3
            else:
                if j % 2 == 0:
                    st["pair_bank"] = prepare_bank(set(range(nb)) | set(range(4, 4 + nb)))
                bank = st["pair_bank"]
                first = 4 * (j % 2)
            for b in range(nb):
                nc.tensor.transpose(bank[:, first + b, :], e[:, (1 + b) * P : (2 + b) * P], ident_bf[:])
            st["bank", n] = bank

        def t_copy(n):
            qb, hg, j, h = where(n)
            if qb < 4 and j % 2 == 0:
                return
            grp = gpool.tile([P, 2, P, 4], BF16, tag="grp", name="grp", align_bytes=64)
            src = st["bank", n][:].rearrange("p (c t) q -> p c q t", t=4)
            units, u = (8, h // 2) if qb < 4 else (16, h)
            if (u + 1) * VEC_BANKS[qb] // units > u * VEC_BANKS[qb] // units:
                nc.vector.tensor_copy(out=grp[:], in_=src)
            else:
                nc.scalar.copy(out=grp[:], in_=src)
            st["grp", n] = grp

        def t_quantise(n):
            qb, hg, j, h = where(n)
            if qb < 4 and j % 2 == 0:
                return
            codes = cpool.tile([P, 2 * P], U32, tag="codes", name="codes", align_bytes=64)
            scl = cpool.tile([P, 2 * P], U8, tag="scl", name="scl", align_bytes=64)
            nc.vector.quantize_mx(
                out=codes[:].bitcast(FP8X4), scales=scl[:],
                in_=st["grp", n][:].rearrange("p g q t -> p (g q t)"),
            )
            st["codes", n] = (codes, scl)

        def tile_at(s, lag):
            return s - lag if 0 <= s - lag < NT else None

        def group_at(s, off, lo=0, hi=NG):
            g, r = divmod(s - off, GH)
            return g if r == 0 and lo <= g < hi else None

        for s in range(G_QKT, NT + G_OUT):
            n = tile_at(s, 0)
            if n is not None:
                t_scores(n)
            n = tile_at(s, LAG_TR)
            if n is not None:
                t_transpose(n)
            g = group_at(s, G_QKT)
            if g is not None:
                g_qk_transpose(g)
            g = group_at(s, G_W, lo=16)
            if g is not None:
                g_window_scores(g)
            g = group_at(s, G_MX)
            if g is not None:
                g_mx(g)
            g = group_at(s, G_BIAS, hi=4)
            if g is not None:
                g_bias(g)
            g = group_at(s, G_QKCOPY)
            if g is not None:
                g_qk_copy(g)
            g = group_at(s, G_WPASS, lo=16)
            if g is not None:
                g_window_pass(g)
            n = tile_at(s, LAG_PASS)
            if n is not None:
                t_pass(n)
            n = tile_at(s, LAG_EXP)
            if n is not None:
                t_exp(n)
            n = tile_at(s, LAG_COPY)
            if n is not None:
                t_copy(n)
            n = tile_at(s, LAG_Q)
            if n is not None:
                t_quantise(n)
            g = group_at(s, G_V)
            if g is not None and g % 16 < 4:
                g_v(g)
            g = group_at(s, G_VQ)
            if g is not None and g % 16 < 4:
                g_v_quantise(g)
            g = group_at(s, G_OUT)
            if g is not None:
                g_out(g)
            if s % H == 6 and N_X <= s // H + N_X < NQB:
                load_x(s // H + N_X)
